import numpy as np
import ml_dtypes


def mxq(x, axis, fmt="e4m3"):
    dtype, down = {"e4m3": (ml_dtypes.float8_e4m3fn, 7), "e5m2": (ml_dtypes.float8_e5m2, 14)}[fmt]
    v = np.moveaxis(np.asarray(x, np.float32).astype(ml_dtypes.bfloat16).astype(np.float64), axis, -1)
    blocks = v.reshape(v.shape[:-1] + (-1, 32))
    amax = np.abs(blocks).max(-1, keepdims=True)
    byte = np.maximum(np.where(amax > 0, np.frexp(amax)[1] - 1 + 127, 0) - down, 1)
    scale = np.exp2(byte - 127.0)
    codes = (blocks / scale).astype(np.float32).astype(dtype).astype(np.float64)
    return np.moveaxis((codes * scale).reshape(v.shape), -1, axis)


WIDE = False


def mx_kscale(k):
    if not WIDE:
        return np.ones(k)
    levels = np.array([10, -10, 5, -5, 0])
    a = np.random.permutation(np.resize(levels, k // 512 * 4)).reshape(k // 512, 4)
    idx = np.arange(k)
    return np.exp2(a[idx // 512, idx % 128 // 32])


BF16 = ml_dtypes.bfloat16


def bf(x):
    return np.asarray(x, np.float32).astype(BF16)


def f64(x):
    return np.asarray(x).astype(np.float64)


N, L, H, E, HEADS, R = 512, 4, 512, 512, 6, 4
EPS = 1e-12


def l2norm(v):
    n = np.sqrt((v * v).sum(-1, keepdims=True))
    return v / np.maximum(n, EPS)


def setup_inputs():
    s = mx_kscale(H)
    gloss = np.random.standard_normal((N, 1, H))
    amp_w = 0.5 + np.random.random_sample((N, L, 1))
    amp_s = 0.5 + np.random.random_sample((N, 1))
    feature = amp_w * 0.7 * (gloss + np.random.standard_normal((N, L, H)))
    aspect_v = amp_s * np.random.standard_normal((N, H))
    return {"feature": bf(feature * s), "aspect_v": bf(aspect_v * s),
            "W": bf(np.random.standard_normal((HEADS, E, H)) / np.sqrt(H) / s),
            "b": bf(0.2 * np.random.standard_normal((HEADS, E)))}


def reference(feature, aspect_v, W, b):
    wt = mxq(f64(W).transpose(0, 2, 1), 1, "e4m3")
    bias = f64(b)
    q = (mxq(f64(aspect_v), 1, "e4m3") @ wt) + bias[:, None, :]
    fh = (mxq(f64(feature), 2, "e4m3").reshape(N * L, H) @ wt).reshape(HEADS, N, L, E) + bias[:, None, None, :]
    return l2norm(q), l2norm(fh).mean(axis=2)

@@ -1,0 +1,193 @@
+from contextlib import ExitStack
+
+import concourse.mybir as mybir
+from concourse.masks import make_identity
+
+F32 = mybir.dt.float32
+BF16 = mybir.dt.bfloat16
+U32 = mybir.dt.uint32
+U8 = mybir.dt.uint8
+FP8X4 = mybir.dt.float8_e4m3fn_x4
+ALU = mybir.AluOpType
+ACT = mybir.ActivationFunctionType
+
+P = 128
+PACK = 4
+SENSES, WORDS, K = 512, 4, 512
+HEADS, E = 6, 512
+EPS = 1e-12
+
+BLOCKS = 4
+HALVES = 2
+SENSE_BLOCKS = SENSES // P
+GROUPS = HEADS * SENSE_BLOCKS
+TILES = 1 + WORDS
+LAG = 2
+FIRST_PIECES = 3
+TURN_STEP = 1
+FIRST_ADD_STEP = 3
+
+FLOPS = 2 * (SENSES + SENSES * WORDS) * K * HEADS * E
+
+
+def tile_biencodermodel_pa_kernel(tc, feature, aspect_v, W, b, out_0, out_1):
+    nc = tc.nc
+    with ExitStack() as ctx:
+        consts = ctx.enter_context(tc.tile_pool(name="consts", bufs=1))
+        operands = ctx.enter_context(tc.tile_pool(name="operands", bufs=1))
+        staging = ctx.enter_context(tc.tile_pool(name="staging", bufs=FIRST_PIECES))
+        vectors = ctx.enter_context(tc.tile_pool(name="vectors", bufs=(LAG + 1) * TILES))
+        squares = ctx.enter_context(tc.tile_pool(name="squares", bufs=4))
+        norms = ctx.enter_context(tc.tile_pool(name="norms", bufs=LAG + 2))
+        results = ctx.enter_context(tc.tile_pool(name="results", bufs=3))
+        turn_psum = ctx.enter_context(tc.psum_pool(name="turn_psum", bufs=2))
+        mx_psum = ctx.enter_context(tc.psum_pool(name="mx_psum", bufs=6))
+        ctx.enter_context(tc.manual_schedule())
+
+        def load_piece(rows, name):
+            raw = operands.tile([P, BLOCKS * K], BF16, name="raw_" + name)
+            nc.sync.dma_start(out=raw[:].rearrange("p (c k) -> p c k", c=BLOCKS), in_=rows)
+            codes = operands.tile([P, BLOCKS * P], U32, name="codes_" + name, align_bytes=64)
+            scales = operands.tile([P, BLOCKS * P], U8, name="scales_" + name, align_bytes=64)
+            return {"raw": raw, "codes": codes, "scales": scales}
+
+        def load_weights(h):
+            return load_piece(W[h].rearrange("(c p) k -> p c k", p=P), "w%d" % h)
+
+        def load_words(i):
+            return load_piece(feature[i * P : (i + 1) * P], "f%d" % i)
+
+        weights = [load_weights(0)]
+        words = [load_words(0)]
+        senses = load_piece(aspect_v.rearrange("(c p) k -> p c k", p=P), "a")
+        bias = consts.tile([P, HEADS * E], BF16)
+        nc.scalar.dma_start(out=bias[:], in_=b.rearrange("h e -> (h e)").partition_broadcast(P))
+        words += [load_words(i) for i in range(1, SENSE_BLOCKS)]
+        weights += [load_weights(h) for h in range(1, HEADS)]
+        pieces = [weights[0], words[0], senses] + words[1:] + weights[1:]
+
+        identity = consts.tile([P, P], F32)
+        make_identity(nc, identity[:])
+        minus_half = consts.tile([P, TILES], F32)
+        nc.gpsimd.memset(minus_half[:], -0.5)
+
+        def turn(piece):
+            row_words = piece["raw"][:].bitcast(F32)
+            grouped = staging.tile([P, BLOCKS * P * PACK], BF16, align_bytes=64)
+            grouped_words = grouped[:].bitcast(F32).rearrange(
+                "p (c r u) -> p c r u", c=BLOCKS, u=HALVES
+            )
+            for pair in range(BLOCKS // 2):
+                turned = turn_psum.tile([P, 2, HALVES, P], F32)
+                for c in range(2):
+                    for u in range(HALVES):
+                        first = ((2 * pair + c) * HALVES + u) * P
+                        nc.tensor.transpose(
+                            turned[:, c, u, :], row_words[:, first : first + P], identity[:]
+                        )
+                nc.scalar.copy(
+                    out=grouped_words[:, 2 * pair : 2 * pair + 2],
+                    in_=turned[:].rearrange("p c u r -> p c r u"),
+                )
+            return grouped
+
+        def quantise(piece, grouped):
+            nc.vector.quantize_mx(
+                out=piece["codes"][:].bitcast(FP8X4), scales=piece["scales"][:], in_=grouped[:]
+            )
+
+        def project(group, g, t):
+            h, i = divmod(g, SENSE_BLOCKS)
+            rows, block = (senses, i) if t == 0 else (words[i], t - 1)
+            cols = slice(block * P, (block + 1) * P)
+            product = mx_psum.tile([P, E], F32)
+            nc.tensor.matmul_mx(
+                out=product[:],
+                lhsT=rows["codes"][:, cols].bitcast(FP8X4),
+                lhsT_scale=rows["scales"][:, cols],
+                rhs=weights[h]["codes"][:].bitcast(FP8X4),
+                rhs_scale=weights[h]["scales"][:],
+                start=True,
+                stop=True,
+            )
+            vector = vectors.tile([P, E], F32)
+            nc.vector.tensor_tensor(
+                out=vector[:], in0=product[:], in1=bias[:, h * E : (h + 1) * E], op=ALU.add
+            )
+            unread = squares.tile([P, E], F32)
+            nc.scalar.activation(
+                out=unread[:],
+                in_=vector[:],
+                func=ACT.Square,
+                accum_out=group["sum_squares"][:, t : t + 1],
+            )
+            group["vectors"].append(vector)
+
+        def invert_norms(group):
+            clamped = norms.tile([P, TILES], F32)
+            nc.gpsimd.tensor_scalar(
+                out=clamped[:], in0=group["sum_squares"][:], scalar1=EPS * EPS, scalar2=None, op0=ALU.max
+            )
+            inverse = norms.tile([P, TILES], F32)
+            nc.gpsimd.tensor_tensor(out=inverse[:], in0=clamped[:], in1=minus_half[:], op=ALU.pow)
+            mean_weight = norms.tile([P, WORDS], F32)
+            nc.gpsimd.tensor_scalar(
+                out=mean_weight[:], in0=inverse[:, 1:TILES], scalar1=1.0 / WORDS, scalar2=None, op0=ALU.mult
+            )
+            group["inverse"] = inverse
+            group["mean_weight"] = mean_weight
+
+        def finish(group, g, step):
+            h, i = divmod(g, SENSE_BLOCKS)
+            sense_rows = slice(i * P, (i + 1) * P)
+            if step == 0:
+                mean = results.tile([P, E], F32)
+                nc.scalar.activation(
+                    out=mean[:],
+                    in_=group["vectors"][1][:],
+                    func=ACT.Copy,
+                    scale=group["mean_weight"][:, 0:1],
+                )
+                group["mean"] = mean
+            elif step == 1:
+                unit = results.tile([P, E], F32)
+                nc.scalar.activation(
+                    out=unit[:], in_=group["vectors"][0][:], func=ACT.Copy, scale=group["inverse"][:, 0:1]
+                )
+                nc.sync.dma_start(out=out_0[h, sense_rows, :], in_=unit[:])
+            elif step >= FIRST_ADD_STEP:
+                word = 1 + step - FIRST_ADD_STEP
+                mean = group["mean"]
+                nc.vector.scalar_tensor_tensor(
+                    out=mean[:],
+                    in0=group["vectors"][1 + word][:],
+                    scalar=group["mean_weight"][:, word : word + 1],
+                    in1=mean[:],
+                    op0=ALU.mult,
+                    op1=ALU.add,
+                )
+                if word == WORDS - 1:
+                    nc.sync.dma_start(out=out_1[h, sense_rows, :], in_=mean[:])
+
+        first_pieces = pieces[:FIRST_PIECES]
+        first_grouped = [turn(piece) for piece in first_pieces]
+        for piece, grouped in zip(first_pieces, first_grouped):
+            quantise(piece, grouped)
+
+        groups = []
+        for g in range(GROUPS + LAG):
+            if g < GROUPS:
+                sum_squares = norms.tile([P, TILES], F32)
+                groups.append({"sum_squares": sum_squares, "vectors": []})
+            piece = pieces[FIRST_PIECES + g] if FIRST_PIECES + g < len(pieces) else None
+            for t in range(FIRST_ADD_STEP + WORDS - 1):
+                if g >= LAG:
+                    finish(groups[g - LAG], g - LAG, t)
+                if g < GROUPS and t < TILES:
+                    project(groups[g], g, t)
+                if piece is not None and t == TURN_STEP:
+                    grouped = turn(piece)
+            if g < GROUPS:
+                invert_norms(groups[g])
+            if piece is not None:
+                quantise(piece, grouped)

@@ -22,7 +22,8 @@ HALVES = 2
 SENSE_BLOCKS = SENSES // P
 GROUPS = HEADS * SENSE_BLOCKS
 TILES = 1 + WORDS
-LAG = 2
+LAG = 3
+TENSOR_WORDS = 2
 FIRST_PIECES = 3
 TURN_STEP = 1
 FIRST_ADD_STEP = 3
@@ -39,9 +40,11 @@ def tile_biencodermodel_pa_kernel(tc, feature, aspect_v, W, b, out_0, out_1):
         vectors = ctx.enter_context(tc.tile_pool(name="vectors", bufs=(LAG + 1) * TILES))
         squares = ctx.enter_context(tc.tile_pool(name="squares", bufs=4))
         norms = ctx.enter_context(tc.tile_pool(name="norms", bufs=LAG + 2))
-        results = ctx.enter_context(tc.tile_pool(name="results", bufs=3))
+        diagonals = ctx.enter_context(tc.tile_pool(name="diagonals", bufs=(LAG + 1) * TENSOR_WORDS))
+        results = ctx.enter_context(tc.tile_pool(name="results", bufs=4))
         turn_psum = ctx.enter_context(tc.psum_pool(name="turn_psum", bufs=2))
-        mx_psum = ctx.enter_context(tc.psum_pool(name="mx_psum", bufs=6))
+        sum_psum = ctx.enter_context(tc.psum_pool(name="sum_psum", bufs=2))
+        mx_psum = ctx.enter_context(tc.psum_pool(name="mx_psum", bufs=4))
         ctx.enter_context(tc.manual_schedule())
 
         def load_piece(rows, name):
@@ -136,19 +139,33 @@ def tile_biencodermodel_pa_kernel(tc, feature, aspect_v, W, b, out_0, out_1):
             )
             group["inverse"] = inverse
             group["mean_weight"] = mean_weight
+            group["diagonals"] = []
+            for word in range(WORDS - TENSOR_WORDS, WORDS):
+                diagonal = diagonals.tile([P, P], F32)
+                nc.gpsimd.tensor_scalar(
+                    out=diagonal[:],
+                    in0=identity[:],
+                    scalar1=mean_weight[:, word : word + 1],
+                    scalar2=0.0,
+                    op0=ALU.mult,
+                    op1=ALU.add,
+                )
+                group["diagonals"].append(diagonal)
 
         def finish(group, g, step):
             h, i = divmod(g, SENSE_BLOCKS)
             sense_rows = slice(i * P, (i + 1) * P)
             if step == 0:
-                mean = results.tile([P, E], F32)
-                nc.scalar.activation(
-                    out=mean[:],
-                    in_=group["vectors"][1][:],
-                    func=ACT.Copy,
-                    scale=group["mean_weight"][:, 0:1],
-                )
-                group["mean"] = mean
+                last_words = sum_psum.tile([P, E], F32)
+                for n in range(TENSOR_WORDS):
+                    nc.tensor.matmul(
+                        out=last_words[:],
+                        lhsT=group["diagonals"][n][:],
+                        rhs=group["vectors"][1 + WORDS - TENSOR_WORDS + n][:],
+                        start=(n == 0),
+                        stop=(n == TENSOR_WORDS - 1),
+                    )
+                group["mean"] = last_words
             elif step == 1:
                 unit = results.tile([P, E], F32)
                 nc.scalar.activation(
@@ -156,17 +173,18 @@ def tile_biencodermodel_pa_kernel(tc, feature, aspect_v, W, b, out_0, out_1):
                 )
                 nc.sync.dma_start(out=out_0[h, sense_rows, :], in_=unit[:])
             elif step >= FIRST_ADD_STEP:
-                word = 1 + step - FIRST_ADD_STEP
-                mean = group["mean"]
+                word = step - FIRST_ADD_STEP
+                mean = results.tile([P, E], F32)
                 nc.vector.scalar_tensor_tensor(
                     out=mean[:],
                     in0=group["vectors"][1 + word][:],
                     scalar=group["mean_weight"][:, word : word + 1],
-                    in1=mean[:],
+                    in1=group["mean"][:],
                     op0=ALU.mult,
                     op1=ALU.add,
                 )
-                if word == WORDS - 1:
+                group["mean"] = mean
+                if word == WORDS - TENSOR_WORDS - 1:
                     nc.sync.dma_start(out=out_1[h, sense_rows, :], in_=mean[:])
 
         first_pieces = pieces[:FIRST_PIECES]
@@ -180,10 +198,10 @@ def tile_biencodermodel_pa_kernel(tc, feature, aspect_v, W, b, out_0, out_1):
                 sum_squares = norms.tile([P, TILES], F32)
                 groups.append({"sum_squares": sum_squares, "vectors": []})
             piece = pieces[FIRST_PIECES + g] if FIRST_PIECES + g < len(pieces) else None
-            for t in range(FIRST_ADD_STEP + WORDS - 1):
+            for t in range(TILES):
                 if g >= LAG:
                     finish(groups[g - LAG], g - LAG, t)
-                if g < GROUPS and t < TILES:
+                if g < GROUPS:
                     project(groups[g], g, t)
                 if piece is not None and t == TURN_STEP:
                     grouped = turn(piece)

@@ -25,8 +25,7 @@ TILES = 1 + WORDS
 LAG = 3
 TENSOR_WORDS = 2
 FIRST_PIECES = 3
-TURN_STEP = 1
-FIRST_ADD_STEP = 3
+RUNS = ((0, 1), (2, 3, 4))
 
 FLOPS = 2 * (SENSES + SENSES * WORDS) * K * HEADS * E
 
@@ -42,9 +41,8 @@ def tile_biencodermodel_pa_kernel(tc, feature, aspect_v, W, b, out_0, out_1):
         norms = ctx.enter_context(tc.tile_pool(name="norms", bufs=LAG + 2))
         diagonals = ctx.enter_context(tc.tile_pool(name="diagonals", bufs=(LAG + 1) * TENSOR_WORDS))
         results = ctx.enter_context(tc.tile_pool(name="results", bufs=4))
-        turn_psum = ctx.enter_context(tc.psum_pool(name="turn_psum", bufs=2))
+        psum = ctx.enter_context(tc.psum_pool(name="psum", bufs=6))
         sum_psum = ctx.enter_context(tc.psum_pool(name="sum_psum", bufs=2))
-        mx_psum = ctx.enter_context(tc.psum_pool(name="mx_psum", bufs=4))
         ctx.enter_context(tc.manual_schedule())
 
         def load_piece(rows, name):
@@ -81,7 +79,7 @@ def tile_biencodermodel_pa_kernel(tc, feature, aspect_v, W, b, out_0, out_1):
                 "p (c r u) -> p c r u", c=BLOCKS, u=HALVES
             )
             for pair in range(BLOCKS // 2):
-                turned = turn_psum.tile([P, 2, HALVES, P], F32)
+                turned = psum.tile([P, 2, HALVES, P], F32, tag="bank")
                 for c in range(2):
                     for u in range(HALVES):
                         first = ((2 * pair + c) * HALVES + u) * P
@@ -99,11 +97,11 @@ def tile_biencodermodel_pa_kernel(tc, feature, aspect_v, W, b, out_0, out_1):
                 out=piece["codes"][:].bitcast(FP8X4), scales=piece["scales"][:], in_=grouped[:]
             )
 
-        def project(group, g, t):
+        def multiply(group, g, t):
             h, i = divmod(g, SENSE_BLOCKS)
             rows, block = (senses, i) if t == 0 else (words[i], t - 1)
             cols = slice(block * P, (block + 1) * P)
-            product = mx_psum.tile([P, E], F32)
+            product = psum.tile([P, E], F32, tag="bank")
             nc.tensor.matmul_mx(
                 out=product[:],
                 lhsT=rows["codes"][:, cols].bitcast(FP8X4),
@@ -113,9 +111,16 @@ def tile_biencodermodel_pa_kernel(tc, feature, aspect_v, W, b, out_0, out_1):
                 start=True,
                 stop=True,
             )
+            group["products"][t] = product
+
+        def add_bias(group, g, t):
+            h = g // SENSE_BLOCKS
             vector = vectors.tile([P, E], F32)
             nc.vector.tensor_tensor(
-                out=vector[:], in0=product[:], in1=bias[:, h * E : (h + 1) * E], op=ALU.add
+                out=vector[:],
+                in0=group["products"][t][:],
+                in1=bias[:, h * E : (h + 1) * E],
+                op=ALU.add,
             )
             unread = squares.tile([P, E], F32)
             nc.scalar.activation(
@@ -124,7 +129,7 @@ def tile_biencodermodel_pa_kernel(tc, feature, aspect_v, W, b, out_0, out_1):
                 func=ACT.Square,
                 accum_out=group["sum_squares"][:, t : t + 1],
             )
-            group["vectors"].append(vector)
+            group["vectors"][t] = vector
 
         def invert_norms(group):
             clamped = norms.tile([P, TILES], F32)
@@ -152,40 +157,41 @@ def tile_biencodermodel_pa_kernel(tc, feature, aspect_v, W, b, out_0, out_1):
                 )
                 group["diagonals"].append(diagonal)
 
-        def finish(group, g, step):
-            h, i = divmod(g, SENSE_BLOCKS)
-            sense_rows = slice(i * P, (i + 1) * P)
-            if step == 0:
-                last_words = sum_psum.tile([P, E], F32)
-                for n in range(TENSOR_WORDS):
-                    nc.tensor.matmul(
-                        out=last_words[:],
-                        lhsT=group["diagonals"][n][:],
-                        rhs=group["vectors"][1 + WORDS - TENSOR_WORDS + n][:],
-                        start=(n == 0),
-                        stop=(n == TENSOR_WORDS - 1),
-                    )
-                group["mean"] = last_words
-            elif step == 1:
-                unit = results.tile([P, E], F32)
-                nc.scalar.activation(
-                    out=unit[:], in_=group["vectors"][0][:], func=ACT.Copy, scale=group["inverse"][:, 0:1]
+        def sum_last_words(group):
+            last_words = sum_psum.tile([P, E], F32)
+            for n in range(TENSOR_WORDS):
+                nc.tensor.matmul(
+                    out=last_words[:],
+                    lhsT=group["diagonals"][n][:],
+                    rhs=group["vectors"][1 + WORDS - TENSOR_WORDS + n][:],
+                    start=(n == 0),
+                    stop=(n == TENSOR_WORDS - 1),
                 )
-                nc.sync.dma_start(out=out_0[h, sense_rows, :], in_=unit[:])
-            elif step >= FIRST_ADD_STEP:
-                word = step - FIRST_ADD_STEP
-                mean = results.tile([P, E], F32)
-                nc.vector.scalar_tensor_tensor(
-                    out=mean[:],
-                    in0=group["vectors"][1 + word][:],
-                    scalar=group["mean_weight"][:, word : word + 1],
-                    in1=group["mean"][:],
-                    op0=ALU.mult,
-                    op1=ALU.add,
-                )
-                group["mean"] = mean
-                if word == WORDS - TENSOR_WORDS - 1:
-                    nc.sync.dma_start(out=out_1[h, sense_rows, :], in_=mean[:])
+            group["mean"] = last_words
+
+        def add_word(group, word):
+            mean = results.tile([P, E], F32)
+            nc.vector.scalar_tensor_tensor(
+                out=mean[:],
+                in0=group["vectors"][1 + word][:],
+                scalar=group["mean_weight"][:, word : word + 1],
+                in1=group["mean"][:],
+                op0=ALU.mult,
+                op1=ALU.add,
+            )
+            group["mean"] = mean
+
+        def scale_senses(group):
+            unit = results.tile([P, E], F32)
+            nc.gpsimd.tensor_scalar(
+                out=unit[:],
+                in0=group["vectors"][0][:],
+                scalar1=group["inverse"][:, 0:1],
+                scalar2=0.0,
+                op0=ALU.mult,
+                op1=ALU.add,
+            )
+            return unit
 
         first_pieces = pieces[:FIRST_PIECES]
         first_grouped = [turn(piece) for piece in first_pieces]
@@ -194,18 +200,35 @@ def tile_biencodermodel_pa_kernel(tc, feature, aspect_v, W, b, out_0, out_1):
 
         groups = []
         for g in range(GROUPS + LAG):
+            new = None
             if g < GROUPS:
                 sum_squares = norms.tile([P, TILES], F32)
-                groups.append({"sum_squares": sum_squares, "vectors": []})
+                new = {"sum_squares": sum_squares, "products": {}, "vectors": {}}
+                groups.append(new)
+            old = groups[g - LAG] if g >= LAG else None
+            if old is not None:
+                old_h, old_i = divmod(g - LAG, SENSE_BLOCKS)
+                old_rows = slice(old_i * P, (old_i + 1) * P)
             piece = pieces[FIRST_PIECES + g] if FIRST_PIECES + g < len(pieces) else None
-            for t in range(TILES):
-                if g >= LAG:
-                    finish(groups[g - LAG], g - LAG, t)
-                if g < GROUPS:
-                    project(groups[g], g, t)
-                if piece is not None and t == TURN_STEP:
-                    grouped = turn(piece)
-            if g < GROUPS:
-                invert_norms(groups[g])
+
+            if old is not None:
+                sum_last_words(old)
+            for run in RUNS:
+                if new is not None:
+                    for t in run:
+                        multiply(new, g, t)
+                    for t in reversed(run):
+                        add_bias(new, g, t)
+                if old is not None:
+                    add_word(old, RUNS.index(run))
+                if run == RUNS[0]:
+                    if old is not None:
+                        nc.sync.dma_start(out=out_0[old_h, old_rows, :], in_=scale_senses(old)[:])
+                    if piece is not None:
+                        grouped = turn(piece)
+            if old is not None:
+                nc.sync.dma_start(out=out_1[old_h, old_rows, :], in_=old["mean"][:])
+            if new is not None:
+                invert_norms(new)
             if piece is not None:
                 quantise(piece, grouped)

@@ -183,13 +183,8 @@ def tile_biencodermodel_pa_kernel(tc, feature, aspect_v, W, b, out_0, out_1):
 
         def scale_senses(group):
             unit = results.tile([P, E], F32)
-            nc.gpsimd.tensor_scalar(
-                out=unit[:],
-                in0=group["vectors"][0][:],
-                scalar1=group["inverse"][:, 0:1],
-                scalar2=0.0,
-                op0=ALU.mult,
-                op1=ALU.add,
+            nc.scalar.activation(
+                out=unit[:], in_=group["vectors"][0][:], func=ACT.Copy, scale=group["inverse"][:, 0:1]
             )
             return unit
 

from contextlib import ExitStack

import concourse.mybir as mybir
from concourse.masks import make_identity

F32 = mybir.dt.float32
BF16 = mybir.dt.bfloat16
U32 = mybir.dt.uint32
U8 = mybir.dt.uint8
FP8X4 = mybir.dt.float8_e4m3fn_x4
ALU = mybir.AluOpType
ACT = mybir.ActivationFunctionType

P = 128
PACK = 4
SENSES, WORDS, K = 512, 4, 512
HEADS, E = 6, 512
EPS = 1e-12

BLOCKS = 4
HALVES = 2
SENSE_BLOCKS = SENSES // P
GROUPS = HEADS * SENSE_BLOCKS
TILES = 1 + WORDS
LAG = 3
TENSOR_WORDS = 2
FIRST_PIECES = 3
RUNS = ((0, 1), (2, 3, 4))

FLOPS = 2 * (SENSES + SENSES * WORDS) * K * HEADS * E


def tile_biencodermodel_pa_kernel(tc, feature, aspect_v, W, b, out_0, out_1):
    nc = tc.nc
    with ExitStack() as ctx:
        consts = ctx.enter_context(tc.tile_pool(name="consts", bufs=1))
        operands = ctx.enter_context(tc.tile_pool(name="operands", bufs=1))
        staging = ctx.enter_context(tc.tile_pool(name="staging", bufs=FIRST_PIECES))
        vectors = ctx.enter_context(tc.tile_pool(name="vectors", bufs=(LAG + 1) * TILES))
        squares = ctx.enter_context(tc.tile_pool(name="squares", bufs=4))
        norms = ctx.enter_context(tc.tile_pool(name="norms", bufs=LAG + 2))
        diagonals = ctx.enter_context(tc.tile_pool(name="diagonals", bufs=(LAG + 1) * TENSOR_WORDS))
        results = ctx.enter_context(tc.tile_pool(name="results", bufs=4))
        psum = ctx.enter_context(tc.psum_pool(name="psum", bufs=6))
        sum_psum = ctx.enter_context(tc.psum_pool(name="sum_psum", bufs=2))
        ctx.enter_context(tc.manual_schedule())

        def load_piece(rows, name):
            raw = operands.tile([P, BLOCKS * K], BF16, name="raw_" + name)
            nc.sync.dma_start(out=raw[:].rearrange("p (c k) -> p c k", c=BLOCKS), in_=rows)
            codes = operands.tile([P, BLOCKS * P], U32, name="codes_" + name, align_bytes=64)
            scales = operands.tile([P, BLOCKS * P], U8, name="scales_" + name, align_bytes=64)
            return {"raw": raw, "codes": codes, "scales": scales}

        def load_weights(h):
            return load_piece(W[h].rearrange("(c p) k -> p c k", p=P), "w%d" % h)

        def load_words(i):
            return load_piece(feature[i * P : (i + 1) * P], "f%d" % i)

        weights = [load_weights(0)]
        words = [load_words(0)]
        senses = load_piece(aspect_v.rearrange("(c p) k -> p c k", p=P), "a")
        bias = consts.tile([P, HEADS * E], BF16)
        nc.scalar.dma_start(out=bias[:], in_=b.rearrange("h e -> (h e)").partition_broadcast(P))
        words += [load_words(i) for i in range(1, SENSE_BLOCKS)]
        weights += [load_weights(h) for h in range(1, HEADS)]
        pieces = [weights[0], words[0], senses] + words[1:] + weights[1:]

        identity = consts.tile([P, P], F32)
        make_identity(nc, identity[:])
        minus_half = consts.tile([P, TILES], F32)
        nc.gpsimd.memset(minus_half[:], -0.5)

        def turn(piece):
            row_words = piece["raw"][:].bitcast(F32)
            grouped = staging.tile([P, BLOCKS * P * PACK], BF16, align_bytes=64)
            grouped_words = grouped[:].bitcast(F32).rearrange(
                "p (c r u) -> p c r u", c=BLOCKS, u=HALVES
            )
            for pair in range(BLOCKS // 2):
                turned = psum.tile([P, 2, HALVES, P], F32, tag="bank")
                for c in range(2):
                    for u in range(HALVES):
                        first = ((2 * pair + c) * HALVES + u) * P
                        nc.tensor.transpose(
                            turned[:, c, u, :], row_words[:, first : first + P], identity[:]
                        )
                nc.scalar.copy(
                    out=grouped_words[:, 2 * pair : 2 * pair + 2],
                    in_=turned[:].rearrange("p c u r -> p c r u"),
                )
            return grouped

        def quantise(piece, grouped):
            nc.vector.quantize_mx(
                out=piece["codes"][:].bitcast(FP8X4), scales=piece["scales"][:], in_=grouped[:]
            )

        def multiply(group, g, t):
            h, i = divmod(g, SENSE_BLOCKS)
            rows, block = (senses, i) if t == 0 else (words[i], t - 1)
            cols = slice(block * P, (block + 1) * P)
            product = psum.tile([P, E], F32, tag="bank")
            nc.tensor.matmul_mx(
                out=product[:],
                lhsT=rows["codes"][:, cols].bitcast(FP8X4),
                lhsT_scale=rows["scales"][:, cols],
                rhs=weights[h]["codes"][:].bitcast(FP8X4),
                rhs_scale=weights[h]["scales"][:],
                start=True,
                stop=True,
            )
            group["products"][t] = product

        def add_bias(group, g, t):
            h = g // SENSE_BLOCKS
            vector = vectors.tile([P, E], F32)
            nc.vector.tensor_tensor(
                out=vector[:],
                in0=group["products"][t][:],
                in1=bias[:, h * E : (h + 1) * E],
                op=ALU.add,
            )
            unread = squares.tile([P, E], F32)
            nc.scalar.activation(
                out=unread[:],
                in_=vector[:],
                func=ACT.Square,
                accum_out=group["sum_squares"][:, t : t + 1],
            )
            group["vectors"][t] = vector

        def invert_norms(group):
            clamped = norms.tile([P, TILES], F32)
            nc.gpsimd.tensor_scalar(
                out=clamped[:], in0=group["sum_squares"][:], scalar1=EPS * EPS, scalar2=None, op0=ALU.max
            )
            inverse = norms.tile([P, TILES], F32)
            nc.gpsimd.tensor_tensor(out=inverse[:], in0=clamped[:], in1=minus_half[:], op=ALU.pow)
            mean_weight = norms.tile([P, WORDS], F32)
            nc.gpsimd.tensor_scalar(
                out=mean_weight[:], in0=inverse[:, 1:TILES], scalar1=1.0 / WORDS, scalar2=None, op0=ALU.mult
            )
            group["inverse"] = inverse
            group["mean_weight"] = mean_weight
            group["diagonals"] = []
            for word in range(WORDS - TENSOR_WORDS, WORDS):
                diagonal = diagonals.tile([P, P], F32)
                nc.gpsimd.tensor_scalar(
                    out=diagonal[:],
                    in0=identity[:],
                    scalar1=mean_weight[:, word : word + 1],
                    scalar2=0.0,
                    op0=ALU.mult,
                    op1=ALU.add,
                )
                group["diagonals"].append(diagonal)

        def sum_last_words(group):
            last_words = sum_psum.tile([P, E], F32)
            for n in range(TENSOR_WORDS):
                nc.tensor.matmul(
                    out=last_words[:],
                    lhsT=group["diagonals"][n][:],
                    rhs=group["vectors"][1 + WORDS - TENSOR_WORDS + n][:],
                    start=(n == 0),
                    stop=(n == TENSOR_WORDS - 1),
                )
            group["mean"] = last_words

        def add_word(group, word):
            mean = results.tile([P, E], F32)
            nc.vector.scalar_tensor_tensor(
                out=mean[:],
                in0=group["vectors"][1 + word][:],
                scalar=group["mean_weight"][:, word : word + 1],
                in1=group["mean"][:],
                op0=ALU.mult,
                op1=ALU.add,
            )
            group["mean"] = mean

        def scale_senses(group):
            unit = results.tile([P, E], F32)
            nc.scalar.activation(
                out=unit[:], in_=group["vectors"][0][:], func=ACT.Copy, scale=group["inverse"][:, 0:1]
            )
            return unit

        first_pieces = pieces[:FIRST_PIECES]
        first_grouped = [turn(piece) for piece in first_pieces]
        for piece, grouped in zip(first_pieces, first_grouped):
            quantise(piece, grouped)

        groups = []
        for g in range(GROUPS + LAG):
            new = None
            if g < GROUPS:
                sum_squares = norms.tile([P, TILES], F32)
                new = {"sum_squares": sum_squares, "products": {}, "vectors": {}}
                groups.append(new)
            old = groups[g - LAG] if g >= LAG else None
            if old is not None:
                old_h, old_i = divmod(g - LAG, SENSE_BLOCKS)
                old_rows = slice(old_i * P, (old_i + 1) * P)
            piece = pieces[FIRST_PIECES + g] if FIRST_PIECES + g < len(pieces) else None

            if old is not None:
                sum_last_words(old)
            for run in RUNS:
                if new is not None:
                    for t in run:
                        multiply(new, g, t)
                    for t in reversed(run):
                        add_bias(new, g, t)
                if old is not None:
                    add_word(old, RUNS.index(run))
                if run == RUNS[0]:
                    if old is not None:
                        nc.sync.dma_start(out=out_0[old_h, old_rows, :], in_=scale_senses(old)[:])
                    if piece is not None:
                        grouped = turn(piece)
            if old is not None:
                nc.sync.dma_start(out=out_1[old_h, old_rows, :], in_=old["mean"][:])
            if new is not None:
                invert_norms(new)
            if piece is not None:
                quantise(piece, grouped)
